import numpy as np
import ml_dtypes


def mxq(x, axis, fmt="e4m3"):
    dtype, down = {"e4m3": (ml_dtypes.float8_e4m3fn, 7), "e5m2": (ml_dtypes.float8_e5m2, 14)}[fmt]
    v = np.moveaxis(np.asarray(x, np.float32).astype(ml_dtypes.bfloat16).astype(np.float64), axis, -1)
    blocks = v.reshape(v.shape[:-1] + (-1, 32))
    amax = np.abs(blocks).max(-1, keepdims=True)
    byte = np.maximum(np.where(amax > 0, np.frexp(amax)[1] - 1 + 127, 0) - down, 1)
    scale = np.exp2(byte - 127.0)
    codes = (blocks / scale).astype(np.float32).astype(dtype).astype(np.float64)
    return np.moveaxis((codes * scale).reshape(v.shape), -1, axis)


WIDE = False


def mx_kscale(k):
    if not WIDE:
        return np.ones(k)
    levels = np.array([10, -10, 5, -5, 0])
    if k % 512:
        return np.exp2(np.random.permutation(np.resize(levels, k // 32))).repeat(32)
    a = np.empty((k // 512, 16))
    for p in range(k // 512):
        a[p, :8] = np.random.permutation(np.resize(levels, 8))
        for g in range(8):
            far = levels[np.abs(levels - a[p, g]) >= 10]
            a[p, g + 8] = far[np.random.randint(len(far))]
    return np.exp2(a.ravel()).repeat(32)


BF16 = ml_dtypes.bfloat16


def bf(x):
    return np.asarray(x, np.float32).astype(BF16)


def f64(x):
    return np.asarray(x).astype(np.float64)


B, L, LV, H = 4, 32, 64, 1024
NUM_ITERATIONS = 3
X = 0.25
V = 0.12 * L
A = 0.6 / (np.sqrt(H) * V)


def setup_inputs():
    s = mx_kscale(H)
    return {"text_feat": bf(np.random.standard_normal((B, L, H)) * X * s),
            "vision_proj": bf(np.random.standard_normal((B, 1, H)) * V),
            "Wt": bf(np.random.standard_normal((H, H)) * A / (X * np.sqrt(H)) / s[None, :]),
            "bt": bf(np.random.standard_normal(H) * 0.5 * A)}


def reference(text_feat, vision_proj, Wt, bt):
    vp = f64(vision_proj)
    text_proj = (mxq(f64(text_feat), 2, "e4m3") @ mxq(f64(Wt), 1, "e4m3").T) + f64(bt)
    agreement = np.sum(text_proj * vp, axis=-1, keepdims=True)
    coupling = np.zeros_like(agreement)
    for _ in range(NUM_ITERATIONS - 1):
        coupling = coupling + agreement
    e = np.exp(coupling - coupling.max(axis=1, keepdims=True))
    routing_weights = e / e.sum(axis=1, keepdims=True)
    weighted_vision = routing_weights * vp
    return text_proj, weighted_vision

@@ -1,0 +1,235 @@
+from contextlib import ExitStack
+
+import concourse.masks as masks
+import concourse.mybir as mybir
+
+F32 = mybir.dt.float32
+BF16 = mybir.dt.bfloat16
+U32 = mybir.dt.uint32
+U8 = mybir.dt.uint8
+FP8X4 = mybir.dt.float8_e4m3fn_x4
+ALU = mybir.AluOpType
+ACT = mybir.ActivationFunctionType
+AXIS = mybir.AxisListType
+
+P = 128
+BATCH = 4
+TOKENS = 32
+K = 1024
+H = 1024
+PACK = 4
+K_PASS = P * PACK
+PASSES = K // K_PASS
+WORDS = K // 2
+FLIPS = WORDS // P
+BLOCKS = H // P
+RUN = 2
+RUNS = BLOCKS // RUN
+COUPLING_ROUNDS = 2.0
+HALF = H // 2
+SQUARE = 32
+CHUNK = H // SQUARE
+IDLE_COLUMNS = 512
+IDLE_PASSES = 3
+
+FLOPS = 2 * P * K * H
+
+
+def tile_dynamicroutingfusion_pa_s_kernel(tc, text_feat, vision_proj, Wt, bt, out_0, out_1):
+    nc = tc.nc
+    text_rows = text_feat.rearrange("b l k -> (b l) k")
+    text_proj_out = out_0.rearrange("b l h -> (b l) h")
+    weighted_out = out_1.rearrange("b l h -> (b l) h")
+
+    with ExitStack() as ctx:
+        ctx.enter_context(tc.manual_schedule())
+        keep = ctx.enter_context(tc.tile_pool(name="keep", bufs=1))
+        stage = ctx.enter_context(tc.tile_pool(name="stage", bufs=2 * RUN))
+        flip_banks = ctx.enter_context(tc.psum_pool(name="flip_banks", bufs=4))
+        sum_banks = ctx.enter_context(tc.psum_pool(name="sum_banks", bufs=4))
+
+        x_rows = keep.tile([P, K], BF16)
+        w_rows = keep.tile([P, BLOCKS, K], BF16)
+        seed = keep.tile([P, 2, CHUNK], BF16, align_bytes=64)
+
+        def load_blocks(first, count):
+            nc.sync.dma_start(
+                out=w_rows[:, first : first + count, :],
+                in_=Wt[first * P : (first + count) * P, :].rearrange("(j p) k -> p j k", p=P),
+            )
+
+        nc.scalar.dma_start(out=seed[:, 0, :], in_=vision_proj.rearrange("b o (m e) -> (b o m) e", e=CHUNK))
+        for b in range(BATCH):
+            nc.scalar.dma_start(
+                out=seed[b * SQUARE : (b + 1) * SQUARE, 1, :], in_=bt.rearrange("(m e) -> m e", e=CHUNK)
+            )
+        nc.sync.dma_start(out=x_rows[:], in_=text_rows)
+        for first in range(0, BLOCKS - 2, 2):
+            load_blocks(first, 2)
+        load_blocks(BLOCKS - 2, 1)
+        load_blocks(BLOCKS - 1, 1)
+
+        identity = keep.tile([P, P], F32)
+        masks.make_identity(nc, identity[:])
+        table_warmer = keep.tile([P, 1], F32)
+        nc.vector.memset(table_warmer[:], 0.0)
+        nc.scalar.activation(out=table_warmer[:], in_=table_warmer[:], func=ACT.Exp)
+
+        zeros = keep.tile([P, IDLE_COLUMNS * PACK], BF16, align_bytes=64)
+        zero_codes = keep.tile([P, IDLE_COLUMNS], U32, align_bytes=64)
+        zero_scales = keep.tile([P, IDLE_COLUMNS], U8, align_bytes=64)
+        nc.vector.memset(zeros[:], 0.0)
+        nc.vector.quantize_mx(out=zero_codes[:].bitcast(FP8X4), scales=zero_scales[:], in_=zeros[:])
+
+        def idle_passes():
+            unread = sum_banks.tile([P, IDLE_COLUMNS], F32, tag="sum_bank")
+            for idle_pass in range(IDLE_PASSES):
+                nc.tensor.matmul_mx(
+                    out=unread[:],
+                    lhsT=zero_codes[:, :P].bitcast(FP8X4),
+                    lhsT_scale=zero_scales[:, :P],
+                    rhs=zero_codes[:].bitcast(FP8X4),
+                    rhs_scale=zero_scales[:],
+                    start=True,
+                    stop=True,
+                )
+
+        seed_flipped = keep.tile([P, SQUARE], F32, align_bytes=64)
+        nc.vector.transpose(out=seed_flipped[:], in_=seed[:].rearrange("p w e -> p (w e)").bitcast(F32))
+        seed_repeated = keep.tile([P, SQUARE, SQUARE], F32, align_bytes=64)
+        nc.vector.tensor_copy(
+            out=seed_repeated[:], in_=seed_flipped[:].unsqueeze(2).to_broadcast([P, SQUARE, SQUARE])
+        )
+        both_rows = keep.tile([P, SQUARE, 2, CHUNK], BF16, align_bytes=64)
+        nc.vector.transpose(
+            out=both_rows[:].rearrange("p m w e -> p (m w e)").bitcast(F32),
+            in_=seed_repeated[:].rearrange("p m i -> p (m i)"),
+        )
+        vision_rows = both_rows[:, :, 0, :]
+        bias_rows = both_rows[:, :, 1, :]
+
+        def chunked(columns):
+            return columns.rearrange("p (m e) -> p m e", e=CHUNK)
+
+        x_codes = keep.tile([P, PASSES * P], U32, align_bytes=64)
+        x_scales = keep.tile([P, PASSES * P], U8, align_bytes=64)
+        w_codes = keep.tile([P, BLOCKS, PASSES * P], U32, align_bytes=64)
+        w_scales = keep.tile([P, BLOCKS, PASSES * P], U8, align_bytes=64)
+
+        def flip(rows):
+            words = rows.bitcast(F32)
+            bank = flip_banks.tile([P, FLIPS, P], F32)
+            for j in range(FLIPS):
+                g, u = divmod(j, 2)
+                every_2nd = words[:, g * 2 * P + u : (g + 1) * 2 * P : 2]
+                nc.tensor.transpose(bank[:, j, :], every_2nd, identity[:])
+            grouped = stage.tile([P, PASSES * P * PACK], BF16, align_bytes=64)
+            nc.scalar.copy(
+                out=grouped[:].bitcast(F32).rearrange("p (g r u) -> p g r u", g=PASSES, u=2),
+                in_=bank[:].rearrange("p (g u) r -> p g r u", u=2),
+            )
+            return grouped
+
+        def quantise(grouped, codes, scales):
+            nc.vector.quantize_mx(out=codes.bitcast(FP8X4), scales=scales, in_=grouped[:])
+
+        text_proj = keep.tile([P, H], F32)
+        products = keep.tile([P, H], F32)
+        coupling_parts = keep.tile([P, BLOCKS], F32)
+
+        def multiply(r):
+            sums = sum_banks.tile([P, P], F32, tag="sum_bank")
+            for g in range(PASSES):
+                cols = slice(g * P, (g + 1) * P)
+                nc.tensor.matmul_mx(
+                    out=sums[:],
+                    lhsT=x_codes[:, cols].bitcast(FP8X4),
+                    lhsT_scale=x_scales[:, cols],
+                    rhs=w_codes[:, r, cols].bitcast(FP8X4),
+                    rhs_scale=w_scales[:, r, cols],
+                    start=(g == 0),
+                    stop=(g == PASSES - 1),
+                )
+            nc.vector.scalar_tensor_tensor(
+                out=chunked(products[:, r * P : (r + 1) * P]),
+                in0=chunked(sums[:]),
+                scalar=COUPLING_ROUNDS,
+                in1=vision_rows[:, r * P // CHUNK : (r + 1) * P // CHUNK, :],
+                op0=ALU.mult,
+                op1=ALU.mult,
+                accum_out=coupling_parts[:, r : r + 1],
+            )
+            return sums
+
+        def add_bias(r, sums):
+            nc.vector.tensor_tensor(
+                out=chunked(text_proj[:, r * P : (r + 1) * P]),
+                in0=chunked(sums[:]),
+                in1=bias_rows[:, r * P // CHUNK : (r + 1) * P // CHUNK, :],
+                op=ALU.add,
+            )
+
+        idle_passes()
+        quantise(flip(x_rows[:]), x_codes[:], x_scales[:])
+        idle_passes()
+        last_sums = []
+        for run in range(RUNS + 1):
+            if run < RUNS:
+                blocks = range(run * RUN, (run + 1) * RUN)
+                flipped = [flip(w_rows[:, r, :]) for r in blocks]
+                for r, grouped in zip(blocks, flipped):
+                    quantise(grouped, w_codes[:, r, :], w_scales[:, r, :])
+            if run == 0:
+                idle_passes()
+            if run >= 1:
+                for r in range((run - 1) * RUN, run * RUN):
+                    sums = multiply(r)
+                    if run < RUNS:
+                        add_bias(r, sums)
+                    else:
+                        last_sums.append((r, sums))
+            if run * RUN == BLOCKS // 2:
+                nc.sync.dma_start(out=text_proj_out[:, :HALF], in_=text_proj[:, :HALF])
+
+        own_coupling = keep.tile([P, TOKENS], F32, align_bytes=64)
+        nc.vector.tensor_reduce(
+            out=own_coupling[:],
+            in_=coupling_parts[:].unsqueeze(1).to_broadcast([P, TOKENS, BLOCKS]),
+            axis=AXIS.X,
+            op=ALU.add,
+        )
+        group_coupling = keep.tile([P, TOKENS], F32, align_bytes=64)
+        nc.vector.transpose(out=group_coupling[:], in_=own_coupling[:])
+        minus_max = keep.tile([P, 1], F32)
+        nc.vector.tensor_reduce(
+            out=minus_max[:], in_=group_coupling[:], axis=AXIS.X, op=ALU.max, negate=True
+        )
+        group_exp = keep.tile([P, TOKENS], F32)
+        exp_sum = keep.tile([P, 1], F32)
+        nc.scalar.activation(
+            out=group_exp[:], in_=group_coupling[:], func=ACT.Exp, bias=minus_max[:], accum_out=exp_sum[:]
+        )
+        own_exp = keep.tile([P, 1], F32)
+        nc.scalar.activation(out=own_exp[:], in_=own_coupling[:, 0:1], func=ACT.Exp, bias=minus_max[:])
+        for r, sums in last_sums:
+            add_bias(r, sums)
+        nc.sync.dma_start(out=text_proj_out[:, HALF:], in_=text_proj[:, HALF:])
+        one_over_sum = keep.tile([P, 1], F32)
+        nc.vector.reciprocal(out=one_over_sum[:], in_=exp_sum[:])
+        routing = keep.tile([P, 1], F32)
+        nc.vector.tensor_tensor(out=routing[:], in0=own_exp[:], in1=one_over_sum[:], op=ALU.mult)
+
+        weighted_left = keep.tile([P, HALF], F32)
+        nc.vector.tensor_scalar(
+            out=chunked(weighted_left[:]),
+            in0=vision_rows[:, : HALF // CHUNK, :],
+            scalar1=routing[:],
+            scalar2=None,
+            op0=ALU.mult,
+        )
+        nc.sync.dma_start(out=weighted_out[:, :HALF], in_=weighted_left[:])
+        weighted_right = keep.tile([P, HALF], F32)
+        nc.scalar.activation(
+            out=chunked(weighted_right[:]), in_=vision_rows[:, HALF // CHUNK :, :], func=ACT.Copy, scale=routing[:]
+        )
+        nc.scalar.dma_start(out=weighted_out[:, HALF:], in_=weighted_right[:])

@@ -18,19 +18,16 @@ TOKENS = 32
 K = 1024
 H = 1024
 PACK = 4
-K_PASS = P * PACK
-PASSES = K // K_PASS
+PASSES = K // (P * PACK)
 WORDS = K // 2
 FLIPS = WORDS // P
 BLOCKS = H // P
-RUN = 2
-RUNS = BLOCKS // RUN
+LAST = BLOCKS - 1
 COUPLING_ROUNDS = 2.0
-HALF = H // 2
 SQUARE = 32
 CHUNK = H // SQUARE
-IDLE_COLUMNS = 512
-IDLE_PASSES = 3
+GROUPS = ((0, 2), (2, 2), (4, 2), (6, 1), (7, 1))
+STORE = 256
 
 FLOPS = 2 * P * K * H
 
@@ -44,30 +41,24 @@ def tile_dynamicroutingfusion_pa_s_kernel(tc, text_feat, vision_proj, Wt, bt, ou
     with ExitStack() as ctx:
         ctx.enter_context(tc.manual_schedule())
         keep = ctx.enter_context(tc.tile_pool(name="keep", bufs=1))
-        stage = ctx.enter_context(tc.tile_pool(name="stage", bufs=2 * RUN))
+        stage = ctx.enter_context(tc.tile_pool(name="stage", bufs=2))
         flip_banks = ctx.enter_context(tc.psum_pool(name="flip_banks", bufs=4))
         sum_banks = ctx.enter_context(tc.psum_pool(name="sum_banks", bufs=4))
 
         x_rows = keep.tile([P, K], BF16)
         w_rows = keep.tile([P, BLOCKS, K], BF16)
         seed = keep.tile([P, 2, CHUNK], BF16, align_bytes=64)
-
-        def load_blocks(first, count):
+        nc.sync.dma_start(out=seed[:, 0, :], in_=vision_proj.rearrange("b o (m e) -> (b o m) e", e=CHUNK))
+        for b in range(BATCH):
+            nc.sync.dma_start(
+                out=seed[b * SQUARE : (b + 1) * SQUARE, 1, :], in_=bt.rearrange("(m e) -> m e", e=CHUNK)
+            )
+        nc.sync.dma_start(out=x_rows[:], in_=text_rows)
+        for first, count in GROUPS:
             nc.sync.dma_start(
                 out=w_rows[:, first : first + count, :],
                 in_=Wt[first * P : (first + count) * P, :].rearrange("(j p) k -> p j k", p=P),
             )
-
-        nc.scalar.dma_start(out=seed[:, 0, :], in_=vision_proj.rearrange("b o (m e) -> (b o m) e", e=CHUNK))
-        for b in range(BATCH):
-            nc.scalar.dma_start(
-                out=seed[b * SQUARE : (b + 1) * SQUARE, 1, :], in_=bt.rearrange("(m e) -> m e", e=CHUNK)
-            )
-        nc.sync.dma_start(out=x_rows[:], in_=text_rows)
-        for first in range(0, BLOCKS - 2, 2):
-            load_blocks(first, 2)
-        load_blocks(BLOCKS - 2, 1)
-        load_blocks(BLOCKS - 1, 1)
 
         identity = keep.tile([P, P], F32)
         masks.make_identity(nc, identity[:])
@@ -75,128 +66,147 @@ def tile_dynamicroutingfusion_pa_s_kernel(tc, text_feat, vision_proj, Wt, bt, ou
         nc.vector.memset(table_warmer[:], 0.0)
         nc.scalar.activation(out=table_warmer[:], in_=table_warmer[:], func=ACT.Exp)
 
-        zeros = keep.tile([P, IDLE_COLUMNS * PACK], BF16, align_bytes=64)
-        zero_codes = keep.tile([P, IDLE_COLUMNS], U32, align_bytes=64)
-        zero_scales = keep.tile([P, IDLE_COLUMNS], U8, align_bytes=64)
-        nc.vector.memset(zeros[:], 0.0)
-        nc.vector.quantize_mx(out=zero_codes[:].bitcast(FP8X4), scales=zero_scales[:], in_=zeros[:])
-
-        def idle_passes():
-            unread = sum_banks.tile([P, IDLE_COLUMNS], F32, tag="sum_bank")
-            for idle_pass in range(IDLE_PASSES):
-                nc.tensor.matmul_mx(
-                    out=unread[:],
-                    lhsT=zero_codes[:, :P].bitcast(FP8X4),
-                    lhsT_scale=zero_scales[:, :P],
-                    rhs=zero_codes[:].bitcast(FP8X4),
-                    rhs_scale=zero_scales[:],
-                    start=True,
-                    stop=True,
-                )
-
         seed_flipped = keep.tile([P, SQUARE], F32, align_bytes=64)
-        nc.vector.transpose(out=seed_flipped[:], in_=seed[:].rearrange("p w e -> p (w e)").bitcast(F32))
         seed_repeated = keep.tile([P, SQUARE, SQUARE], F32, align_bytes=64)
-        nc.vector.tensor_copy(
-            out=seed_repeated[:], in_=seed_flipped[:].unsqueeze(2).to_broadcast([P, SQUARE, SQUARE])
-        )
         both_rows = keep.tile([P, SQUARE, 2, CHUNK], BF16, align_bytes=64)
-        nc.vector.transpose(
-            out=both_rows[:].rearrange("p m w e -> p (m w e)").bitcast(F32),
-            in_=seed_repeated[:].rearrange("p m i -> p (m i)"),
-        )
         vision_rows = both_rows[:, :, 0, :]
         bias_rows = both_rows[:, :, 1, :]
+
+        def spread_half(half):
+            m = slice(half * SQUARE // 2, (half + 1) * SQUARE // 2)
+            nc.vector.tensor_copy(
+                out=seed_repeated[:, m, :],
+                in_=seed_flipped[:, m].unsqueeze(2).to_broadcast([P, SQUARE // 2, SQUARE]),
+            )
+            nc.vector.transpose(
+                out=both_rows[:, m, :, :].rearrange("p m w e -> p (m w e)").bitcast(F32),
+                in_=seed_repeated[:, m, :].rearrange("p m i -> p (m i)"),
+            )
 
         def chunked(columns):
             return columns.rearrange("p (m e) -> p m e", e=CHUNK)
 
         x_codes = keep.tile([P, PASSES * P], U32, align_bytes=64)
         x_scales = keep.tile([P, PASSES * P], U8, align_bytes=64)
-        w_codes = keep.tile([P, BLOCKS, PASSES * P], U32, align_bytes=64)
-        w_scales = keep.tile([P, BLOCKS, PASSES * P], U8, align_bytes=64)
+        w_codes = keep.tile([P, PASSES * H], U32, align_bytes=64)
+        w_scales = keep.tile([P, PASSES * H], U8, align_bytes=64)
 
-        def flip(rows):
+        def group_columns(first, count):
+            return slice(first * PASSES * P, (first + count) * PASSES * P)
+
+        def flip(rows, grouped, j, count):
             words = rows.bitcast(F32)
             bank = flip_banks.tile([P, FLIPS, P], F32)
-            for j in range(FLIPS):
-                g, u = divmod(j, 2)
+            for f in range(FLIPS):
+                g, u = divmod(f, 2)
                 every_2nd = words[:, g * 2 * P + u : (g + 1) * 2 * P : 2]
-                nc.tensor.transpose(bank[:, j, :], every_2nd, identity[:])
-            grouped = stage.tile([P, PASSES * P * PACK], BF16, align_bytes=64)
+                nc.tensor.transpose(bank[:, f, :], every_2nd, identity[:])
             nc.scalar.copy(
-                out=grouped[:].bitcast(F32).rearrange("p (g r u) -> p g r u", g=PASSES, u=2),
+                out=grouped[:].bitcast(F32).rearrange("p (g j r u) -> p g j r u", g=PASSES, j=count, u=2)[:, :, j],
                 in_=bank[:].rearrange("p (g u) r -> p g r u", u=2),
             )
+
+        def flip_group(first, count):
+            grouped = stage.tile([P, PASSES * count * P * PACK], BF16, align_bytes=64, tag=f"grouped_{count}")
+            for j in range(count):
+                flip(w_rows[:, first + j, :], grouped, j, count)
             return grouped
 
         def quantise(grouped, codes, scales):
             nc.vector.quantize_mx(out=codes.bitcast(FP8X4), scales=scales, in_=grouped[:])
 
+        def quantise_group(first, count, grouped):
+            cols = group_columns(first, count)
+            quantise(grouped, w_codes[:, cols], w_scales[:, cols])
+
         text_proj = keep.tile([P, H], F32)
         products = keep.tile([P, H], F32)
-        coupling_parts = keep.tile([P, BLOCKS], F32)
+        coupling_parts = keep.tile([P, len(GROUPS)], F32)
 
-        def multiply(r):
-            sums = sum_banks.tile([P, P], F32, tag="sum_bank")
+        def multiply(first, count):
+            sums = sum_banks.tile([P, count * P], F32, tag="sum_bank")
             for g in range(PASSES):
-                cols = slice(g * P, (g + 1) * P)
+                x_cols = slice(g * P, (g + 1) * P)
+                w_cols = slice((first * PASSES + g * count) * P, (first * PASSES + (g + 1) * count) * P)
                 nc.tensor.matmul_mx(
                     out=sums[:],
-                    lhsT=x_codes[:, cols].bitcast(FP8X4),
-                    lhsT_scale=x_scales[:, cols],
-                    rhs=w_codes[:, r, cols].bitcast(FP8X4),
-                    rhs_scale=w_scales[:, r, cols],
+                    lhsT=x_codes[:, x_cols].bitcast(FP8X4),
+                    lhsT_scale=x_scales[:, x_cols],
+                    rhs=w_codes[:, w_cols].bitcast(FP8X4),
+                    rhs_scale=w_scales[:, w_cols],
                     start=(g == 0),
                     stop=(g == PASSES - 1),
                 )
-            nc.vector.scalar_tensor_tensor(
-                out=chunked(products[:, r * P : (r + 1) * P]),
-                in0=chunked(sums[:]),
-                scalar=COUPLING_ROUNDS,
-                in1=vision_rows[:, r * P // CHUNK : (r + 1) * P // CHUNK, :],
-                op0=ALU.mult,
-                op1=ALU.mult,
-                accum_out=coupling_parts[:, r : r + 1],
-            )
             return sums
 
-        def add_bias(r, sums):
-            nc.vector.tensor_tensor(
-                out=chunked(text_proj[:, r * P : (r + 1) * P]),
+        def add_coupling(i, sums):
+            first, count = GROUPS[i]
+            h = slice(first * P, (first + count) * P)
+            nc.vector.scalar_tensor_tensor(
+                out=chunked(products[:, h]),
                 in0=chunked(sums[:]),
-                in1=bias_rows[:, r * P // CHUNK : (r + 1) * P // CHUNK, :],
+                scalar=COUPLING_ROUNDS,
+                in1=vision_rows[:, h.start // CHUNK : h.stop // CHUNK, :],
+                op0=ALU.mult,
+                op1=ALU.mult,
+                accum_out=coupling_parts[:, i : i + 1],
+            )
+
+        def add_bias(i, sums):
+            first, count = GROUPS[i]
+            h = slice(first * P, (first + count) * P)
+            nc.vector.tensor_tensor(
+                out=chunked(text_proj[:, h]),
+                in0=chunked(sums[:]),
+                in1=bias_rows[:, h.start // CHUNK : h.stop // CHUNK, :],
                 op=ALU.add,
             )
 
-        idle_passes()
-        quantise(flip(x_rows[:]), x_codes[:], x_scales[:])
-        idle_passes()
-        last_sums = []
-        for run in range(RUNS + 1):
-            if run < RUNS:
-                blocks = range(run * RUN, (run + 1) * RUN)
-                flipped = [flip(w_rows[:, r, :]) for r in blocks]
-                for r, grouped in zip(blocks, flipped):
-                    quantise(grouped, w_codes[:, r, :], w_scales[:, r, :])
-            if run == 0:
-                idle_passes()
-            if run >= 1:
-                for r in range((run - 1) * RUN, run * RUN):
-                    sums = multiply(r)
-                    if run < RUNS:
-                        add_bias(r, sums)
-                    else:
-                        last_sums.append((r, sums))
-            if run * RUN == BLOCKS // 2:
-                nc.sync.dma_start(out=text_proj_out[:, :HALF], in_=text_proj[:, :HALF])
+        nc.vector.transpose(out=seed_flipped[:], in_=seed[:].rearrange("p w e -> p (w e)").bitcast(F32))
+        spread_half(0)
+        spread_half(1)
+        x_grouped = stage.tile([P, PASSES * P * PACK], BF16, align_bytes=64, tag="grouped_1")
+        flip(x_rows[:], x_grouped, 0, 1)
+        quantise(x_grouped, x_codes[:], x_scales[:])
 
-        own_coupling = keep.tile([P, TOKENS], F32, align_bytes=64)
+        g0 = flip_group(*GROUPS[0])
+        quantise_group(*GROUPS[0], g0)
+        g1 = flip_group(*GROUPS[1])
+        quantise_group(*GROUPS[1], g1)
+        g2 = flip_group(*GROUPS[2])
+        s0 = multiply(*GROUPS[0])
+        add_coupling(0, s0)
+        quantise_group(*GROUPS[2], g2)
+        g3 = flip_group(*GROUPS[3])
+        s1 = multiply(*GROUPS[1])
+        add_bias(0, s0)
+        add_coupling(1, s1)
+        quantise_group(*GROUPS[3], g3)
+        g4 = flip_group(*GROUPS[4])
+        s2 = multiply(*GROUPS[2])
+        add_coupling(2, s2)
+        quantise_group(*GROUPS[4], g4)
+        add_bias(1, s1)
+        nc.sync.dma_start(out=text_proj_out[:, : 4 * P], in_=text_proj[:, : 4 * P])
+        s3 = multiply(*GROUPS[3])
+        s4 = multiply(*GROUPS[4])
+        add_coupling(3, s3)
+
+        early_coupling = keep.tile([P, TOKENS], F32, align_bytes=64)
         nc.vector.tensor_reduce(
-            out=own_coupling[:],
-            in_=coupling_parts[:].unsqueeze(1).to_broadcast([P, TOKENS, BLOCKS]),
+            out=early_coupling[:],
+            in_=coupling_parts[:, : len(GROUPS) - 1].unsqueeze(1).to_broadcast([P, TOKENS, len(GROUPS) - 1]),
             axis=AXIS.X,
             op=ALU.add,
+        )
+        add_coupling(4, s4)
+        own_coupling = keep.tile([P, TOKENS], F32, align_bytes=64)
+        nc.vector.tensor_scalar(
+            out=own_coupling[:],
+            in0=early_coupling[:],
+            scalar1=coupling_parts[:, len(GROUPS) - 1 :],
+            scalar2=None,
+            op0=ALU.add,
         )
         group_coupling = keep.tile([P, TOKENS], F32, align_bytes=64)
         nc.vector.transpose(out=group_coupling[:], in_=own_coupling[:])
@@ -211,25 +221,22 @@ def tile_dynamicroutingfusion_pa_s_kernel(tc, text_feat, vision_proj, Wt, bt, ou
         )
         own_exp = keep.tile([P, 1], F32)
         nc.scalar.activation(out=own_exp[:], in_=own_coupling[:, 0:1], func=ACT.Exp, bias=minus_max[:])
-        for r, sums in last_sums:
-            add_bias(r, sums)
-        nc.sync.dma_start(out=text_proj_out[:, HALF:], in_=text_proj[:, HALF:])
+        add_bias(2, s2)
+        add_bias(3, s3)
+        nc.sync.dma_start(out=text_proj_out[:, 4 * P : 7 * P], in_=text_proj[:, 4 * P : 7 * P])
         one_over_sum = keep.tile([P, 1], F32)
         nc.vector.reciprocal(out=one_over_sum[:], in_=exp_sum[:])
-        routing = keep.tile([P, 1], F32)
-        nc.vector.tensor_tensor(out=routing[:], in0=own_exp[:], in1=one_over_sum[:], op=ALU.mult)
 
-        weighted_left = keep.tile([P, HALF], F32)
-        nc.vector.tensor_scalar(
-            out=chunked(weighted_left[:]),
-            in0=vision_rows[:, : HALF // CHUNK, :],
-            scalar1=routing[:],
-            scalar2=None,
-            op0=ALU.mult,
-        )
-        nc.sync.dma_start(out=weighted_out[:, :HALF], in_=weighted_left[:])
-        weighted_right = keep.tile([P, HALF], F32)
-        nc.scalar.activation(
-            out=chunked(weighted_right[:]), in_=vision_rows[:, HALF // CHUNK :, :], func=ACT.Copy, scale=routing[:]
-        )
-        nc.scalar.dma_start(out=weighted_out[:, HALF:], in_=weighted_right[:])
+        weighted = keep.tile([P, H], F32)
+        for c in range(0, H, STORE):
+            nc.vector.tensor_scalar(
+                out=chunked(weighted[:, c : c + STORE]),
+                in0=vision_rows[:, c // CHUNK : (c + STORE) // CHUNK, :],
+                scalar1=own_exp[:],
+                scalar2=one_over_sum[:],
+                op0=ALU.mult,
+                op1=ALU.mult,
+            )
+            nc.sync.dma_start(out=weighted_out[:, c : c + STORE], in_=weighted[:, c : c + STORE])
+        add_bias(4, s4)
+        nc.sync.dma_start(out=text_proj_out[:, 7 * P :], in_=text_proj[:, 7 * P :])

@@ -22,11 +22,12 @@ PASSES = K // (P * PACK)
 WORDS = K // 2
 FLIPS = WORDS // P
 BLOCKS = H // P
-LAST = BLOCKS - 1
 COUPLING_ROUNDS = 2.0
 SQUARE = 32
 CHUNK = H // SQUARE
+LOADS = ((0, 2), (2, 2), (4, 2), (6, 1), (7, 1))
 GROUPS = ((0, 2), (2, 2), (4, 2), (6, 1), (7, 1))
+EARLY = 3
 STORE = 256
 
 FLOPS = 2 * P * K * H
@@ -41,7 +42,7 @@ def tile_dynamicroutingfusion_pa_s_kernel(tc, text_feat, vision_proj, Wt, bt, ou
     with ExitStack() as ctx:
         ctx.enter_context(tc.manual_schedule())
         keep = ctx.enter_context(tc.tile_pool(name="keep", bufs=1))
-        stage = ctx.enter_context(tc.tile_pool(name="stage", bufs=2))
+        stage = ctx.enter_context(tc.tile_pool(name="stage", bufs=4))
         flip_banks = ctx.enter_context(tc.psum_pool(name="flip_banks", bufs=4))
         sum_banks = ctx.enter_context(tc.psum_pool(name="sum_banks", bufs=4))
 
@@ -54,7 +55,7 @@ def tile_dynamicroutingfusion_pa_s_kernel(tc, text_feat, vision_proj, Wt, bt, ou
                 out=seed[b * SQUARE : (b + 1) * SQUARE, 1, :], in_=bt.rearrange("(m e) -> m e", e=CHUNK)
             )
         nc.sync.dma_start(out=x_rows[:], in_=text_rows)
-        for first, count in GROUPS:
+        for first, count in LOADS:
             nc.sync.dma_start(
                 out=w_rows[:, first : first + count, :],
                 in_=Wt[first * P : (first + count) * P, :].rearrange("(j p) k -> p j k", p=P),
@@ -67,84 +68,83 @@ def tile_dynamicroutingfusion_pa_s_kernel(tc, text_feat, vision_proj, Wt, bt, ou
         nc.scalar.activation(out=table_warmer[:], in_=table_warmer[:], func=ACT.Exp)
 
         seed_flipped = keep.tile([P, SQUARE], F32, align_bytes=64)
+        nc.vector.transpose(out=seed_flipped[:], in_=seed[:].rearrange("p w e -> p (w e)").bitcast(F32))
         seed_repeated = keep.tile([P, SQUARE, SQUARE], F32, align_bytes=64)
+        nc.vector.tensor_copy(
+            out=seed_repeated[:], in_=seed_flipped[:].unsqueeze(2).to_broadcast([P, SQUARE, SQUARE])
+        )
         both_rows = keep.tile([P, SQUARE, 2, CHUNK], BF16, align_bytes=64)
+        nc.vector.transpose(
+            out=both_rows[:].rearrange("p m w e -> p (m w e)").bitcast(F32),
+            in_=seed_repeated[:].rearrange("p m i -> p (m i)"),
+        )
         vision_rows = both_rows[:, :, 0, :]
         bias_rows = both_rows[:, :, 1, :]
-
-        def spread_half(half):
-            m = slice(half * SQUARE // 2, (half + 1) * SQUARE // 2)
-            nc.vector.tensor_copy(
-                out=seed_repeated[:, m, :],
-                in_=seed_flipped[:, m].unsqueeze(2).to_broadcast([P, SQUARE // 2, SQUARE]),
-            )
-            nc.vector.transpose(
-                out=both_rows[:, m, :, :].rearrange("p m w e -> p (m w e)").bitcast(F32),
-                in_=seed_repeated[:, m, :].rearrange("p m i -> p (m i)"),
-            )
 
         def chunked(columns):
             return columns.rearrange("p (m e) -> p m e", e=CHUNK)
 
         x_codes = keep.tile([P, PASSES * P], U32, align_bytes=64)
         x_scales = keep.tile([P, PASSES * P], U8, align_bytes=64)
-        w_codes = keep.tile([P, PASSES * H], U32, align_bytes=64)
-        w_scales = keep.tile([P, PASSES * H], U8, align_bytes=64)
+        w_codes = keep.tile([P, BLOCKS, PASSES * P], U32, align_bytes=64)
+        w_scales = keep.tile([P, BLOCKS, PASSES * P], U8, align_bytes=64)
 
-        def group_columns(first, count):
-            return slice(first * PASSES * P, (first + count) * PASSES * P)
-
-        def flip(rows, grouped, j, count):
+        def flip(rows):
             words = rows.bitcast(F32)
             bank = flip_banks.tile([P, FLIPS, P], F32)
             for f in range(FLIPS):
                 g, u = divmod(f, 2)
                 every_2nd = words[:, g * 2 * P + u : (g + 1) * 2 * P : 2]
                 nc.tensor.transpose(bank[:, f, :], every_2nd, identity[:])
+            grouped = stage.tile([P, PASSES * P * PACK], BF16, align_bytes=64)
             nc.scalar.copy(
-                out=grouped[:].bitcast(F32).rearrange("p (g j r u) -> p g j r u", g=PASSES, j=count, u=2)[:, :, j],
+                out=grouped[:].bitcast(F32).rearrange("p (g r u) -> p g r u", g=PASSES, u=2),
                 in_=bank[:].rearrange("p (g u) r -> p g r u", u=2),
             )
-
-        def flip_group(first, count):
-            grouped = stage.tile([P, PASSES * count * P * PACK], BF16, align_bytes=64, tag=f"grouped_{count}")
-            for j in range(count):
-                flip(w_rows[:, first + j, :], grouped, j, count)
             return grouped
+
+        grouped_blocks = {}
+
+        def flip_block(r):
+            grouped_blocks[r] = flip(w_rows[:, r, :])
 
         def quantise(grouped, codes, scales):
             nc.vector.quantize_mx(out=codes.bitcast(FP8X4), scales=scales, in_=grouped[:])
 
-        def quantise_group(first, count, grouped):
-            cols = group_columns(first, count)
-            quantise(grouped, w_codes[:, cols], w_scales[:, cols])
+        def quantise_block(r):
+            quantise(grouped_blocks[r], w_codes[:, r, :], w_scales[:, r, :])
 
         text_proj = keep.tile([P, H], F32)
         products = keep.tile([P, H], F32)
         coupling_parts = keep.tile([P, len(GROUPS)], F32)
+        group_sums = {}
 
-        def multiply(first, count):
-            sums = sum_banks.tile([P, count * P], F32, tag="sum_bank")
-            for g in range(PASSES):
-                x_cols = slice(g * P, (g + 1) * P)
-                w_cols = slice((first * PASSES + g * count) * P, (first * PASSES + (g + 1) * count) * P)
-                nc.tensor.matmul_mx(
-                    out=sums[:],
-                    lhsT=x_codes[:, x_cols].bitcast(FP8X4),
-                    lhsT_scale=x_scales[:, x_cols],
-                    rhs=w_codes[:, w_cols].bitcast(FP8X4),
-                    rhs_scale=w_scales[:, w_cols],
-                    start=(g == 0),
-                    stop=(g == PASSES - 1),
-                )
-            return sums
+        def multiply(i):
+            first, count = GROUPS[i]
+            if i < len(GROUPS) - 1:
+                sums = sum_banks.tile([P, count * P], F32, tag="sum_bank")
+            else:
+                sums = flip_banks.tile([P, count * P], F32, tag="bank")
+            for j in range(count):
+                for g in range(PASSES):
+                    cols = slice(g * P, (g + 1) * P)
+                    nc.tensor.matmul_mx(
+                        out=sums[:, j * P : (j + 1) * P],
+                        lhsT=x_codes[:, cols].bitcast(FP8X4),
+                        lhsT_scale=x_scales[:, cols],
+                        rhs=w_codes[:, first + j, cols].bitcast(FP8X4),
+                        rhs_scale=w_scales[:, first + j, cols],
+                        start=(g == 0),
+                        stop=(g == PASSES - 1),
+                    )
+            group_sums[i] = sums
 
-        def add_coupling(i, sums):
+        def add_coupling(i):
             first, count = GROUPS[i]
             h = slice(first * P, (first + count) * P)
             nc.vector.scalar_tensor_tensor(
                 out=chunked(products[:, h]),
-                in0=chunked(sums[:]),
+                in0=chunked(group_sums[i][:]),
                 scalar=COUPLING_ROUNDS,
                 in1=vision_rows[:, h.start // CHUNK : h.stop // CHUNK, :],
                 op0=ALU.mult,
@@ -152,64 +152,65 @@ def tile_dynamicroutingfusion_pa_s_kernel(tc, text_feat, vision_proj, Wt, bt, ou
                 accum_out=coupling_parts[:, i : i + 1],
             )
 
-        def add_bias(i, sums):
-            first, count = GROUPS[i]
-            h = slice(first * P, (first + count) * P)
+        def add_bias(r):
+            i = min(r // 2, EARLY) + (r == BLOCKS - 1)
+            here = (r - GROUPS[i][0]) * P
+            h = slice(r * P, (r + 1) * P)
             nc.vector.tensor_tensor(
                 out=chunked(text_proj[:, h]),
-                in0=chunked(sums[:]),
+                in0=chunked(group_sums[i][:, here : here + P]),
                 in1=bias_rows[:, h.start // CHUNK : h.stop // CHUNK, :],
                 op=ALU.add,
             )
+            if h.stop % STORE == 0:
+                done = slice(h.stop - STORE, h.stop)
+                nc.sync.dma_start(out=text_proj_out[:, done], in_=text_proj[:, done])
 
-        nc.vector.transpose(out=seed_flipped[:], in_=seed[:].rearrange("p w e -> p (w e)").bitcast(F32))
-        spread_half(0)
-        spread_half(1)
-        x_grouped = stage.tile([P, PASSES * P * PACK], BF16, align_bytes=64, tag="grouped_1")
-        flip(x_rows[:], x_grouped, 0, 1)
-        quantise(x_grouped, x_codes[:], x_scales[:])
-
-        g0 = flip_group(*GROUPS[0])
-        quantise_group(*GROUPS[0], g0)
-        g1 = flip_group(*GROUPS[1])
-        quantise_group(*GROUPS[1], g1)
-        g2 = flip_group(*GROUPS[2])
-        s0 = multiply(*GROUPS[0])
-        add_coupling(0, s0)
-        quantise_group(*GROUPS[2], g2)
-        g3 = flip_group(*GROUPS[3])
-        s1 = multiply(*GROUPS[1])
-        add_bias(0, s0)
-        add_coupling(1, s1)
-        quantise_group(*GROUPS[3], g3)
-        g4 = flip_group(*GROUPS[4])
-        s2 = multiply(*GROUPS[2])
-        add_coupling(2, s2)
-        quantise_group(*GROUPS[4], g4)
-        add_bias(1, s1)
-        nc.sync.dma_start(out=text_proj_out[:, : 4 * P], in_=text_proj[:, : 4 * P])
-        s3 = multiply(*GROUPS[3])
-        s4 = multiply(*GROUPS[4])
-        add_coupling(3, s3)
+        quantise(flip(x_rows[:]), x_codes[:], x_scales[:])
+        for r in range(4):
+            flip_block(r)
+            quantise_block(r)
+        flip_block(4)
+        flip_block(5)
+        multiply(0)
+        add_coupling(0)
+        quantise_block(4)
+        flip_block(6)
+        multiply(1)
+        quantise_block(5)
+        add_coupling(1)
+        flip_block(7)
+        quantise_block(6)
+        multiply(2)
+        add_coupling(2)
+        quantise_block(7)
+        multiply(3)
+        add_coupling(3)
+        multiply(4)
 
         early_coupling = keep.tile([P, TOKENS], F32, align_bytes=64)
         nc.vector.tensor_reduce(
             out=early_coupling[:],
-            in_=coupling_parts[:, : len(GROUPS) - 1].unsqueeze(1).to_broadcast([P, TOKENS, len(GROUPS) - 1]),
+            in_=coupling_parts[:, :EARLY].unsqueeze(1).to_broadcast([P, TOKENS, EARLY]),
             axis=AXIS.X,
             op=ALU.add,
         )
-        add_coupling(4, s4)
+        add_bias(0)
+        add_coupling(4)
+        add_bias(1)
         own_coupling = keep.tile([P, TOKENS], F32, align_bytes=64)
         nc.vector.tensor_scalar(
             out=own_coupling[:],
             in0=early_coupling[:],
-            scalar1=coupling_parts[:, len(GROUPS) - 1 :],
-            scalar2=None,
+            scalar1=coupling_parts[:, EARLY : EARLY + 1],
+            scalar2=coupling_parts[:, EARLY + 1 : EARLY + 2],
             op0=ALU.add,
+            op1=ALU.add,
         )
+        add_bias(2)
         group_coupling = keep.tile([P, TOKENS], F32, align_bytes=64)
         nc.vector.transpose(out=group_coupling[:], in_=own_coupling[:])
+        add_bias(3)
         minus_max = keep.tile([P, 1], F32)
         nc.vector.tensor_reduce(
             out=minus_max[:], in_=group_coupling[:], axis=AXIS.X, op=ALU.max, negate=True
@@ -221,11 +222,12 @@ def tile_dynamicroutingfusion_pa_s_kernel(tc, text_feat, vision_proj, Wt, bt, ou
         )
         own_exp = keep.tile([P, 1], F32)
         nc.scalar.activation(out=own_exp[:], in_=own_coupling[:, 0:1], func=ACT.Exp, bias=minus_max[:])
-        add_bias(2, s2)
-        add_bias(3, s3)
-        nc.sync.dma_start(out=text_proj_out[:, 4 * P : 7 * P], in_=text_proj[:, 4 * P : 7 * P])
+        add_bias(4)
+        add_bias(5)
+        add_bias(6)
         one_over_sum = keep.tile([P, 1], F32)
         nc.vector.reciprocal(out=one_over_sum[:], in_=exp_sum[:])
+        add_bias(7)
 
         weighted = keep.tile([P, H], F32)
         for c in range(0, H, STORE):
@@ -238,5 +240,3 @@ def tile_dynamicroutingfusion_pa_s_kernel(tc, text_feat, vision_proj, Wt, bt, ou
                 op1=ALU.mult,
             )
             nc.sync.dma_start(out=weighted_out[:, c : c + STORE], in_=weighted[:, c : c + STORE])
-        add_bias(4, s4)
-        nc.sync.dma_start(out=text_proj_out[:, 7 * P :], in_=text_proj[:, 7 * P :])

@@ -29,6 +29,7 @@ LOADS = ((0, 2), (2, 2), (4, 2), (6, 1), (7, 1))
 GROUPS = ((0, 2), (2, 2), (4, 2), (6, 1), (7, 1))
 EARLY = 3
 STORE = 256
+WARM_UPS = 5
 
 FLOPS = 2 * P * K * H
 
@@ -63,6 +64,9 @@ def tile_dynamicroutingfusion_pa_s_kernel(tc, text_feat, vision_proj, Wt, bt, ou
 
         identity = keep.tile([P, P], F32)
         masks.make_identity(nc, identity[:])
+        for warm_up in range(WARM_UPS):
+            unread = sum_banks.tile([P, P], F32, tag="sum_bank")
+            nc.tensor.matmul(out=unread[:], lhsT=identity[:], rhs=identity[:], start=True, stop=True)
         table_warmer = keep.tile([P, 1], F32)
         nc.vector.memset(table_warmer[:], 0.0)
         nc.scalar.activation(out=table_warmer[:], in_=table_warmer[:], func=ACT.Exp)

@@ -28,7 +28,7 @@ CHUNK = H // SQUARE
 LOADS = ((0, 2), (2, 2), (4, 2), (6, 1), (7, 1))
 GROUPS = ((0, 2), (2, 2), (4, 2), (6, 1), (7, 1))
 EARLY = 3
-STORE = 256
+STORE = 512
 WARM_UPS = 5
 
 FLOPS = 2 * P * K * H
@@ -243,4 +243,5 @@ def tile_dynamicroutingfusion_pa_s_kernel(tc, text_feat, vision_proj, Wt, bt, ou
                 op0=ALU.mult,
                 op1=ALU.mult,
             )
-            nc.sync.dma_start(out=weighted_out[:, c : c + STORE], in_=weighted[:, c : c + STORE])
+            queue = nc.scalar if c else nc.sync
+            queue.dma_start(out=weighted_out[:, c : c + STORE], in_=weighted[:, c : c + STORE])

@@ -29,7 +29,7 @@ LOADS = ((0, 2), (2, 2), (4, 2), (6, 1), (7, 1))
 GROUPS = ((0, 2), (2, 2), (4, 2), (6, 1), (7, 1))
 EARLY = 3
 STORE = 512
-WARM_UPS = 5
+WARM_UPS = 3
 
 FLOPS = 2 * P * K * H
 
@@ -78,10 +78,14 @@ def tile_dynamicroutingfusion_pa_s_kernel(tc, text_feat, vision_proj, Wt, bt, ou
             out=seed_repeated[:], in_=seed_flipped[:].unsqueeze(2).to_broadcast([P, SQUARE, SQUARE])
         )
         both_rows = keep.tile([P, SQUARE, 2, CHUNK], BF16, align_bytes=64)
-        nc.vector.transpose(
-            out=both_rows[:].rearrange("p m w e -> p (m w e)").bitcast(F32),
-            in_=seed_repeated[:].rearrange("p m i -> p (m i)"),
-        )
+
+        def spread_half(half):
+            m = slice(half * SQUARE // 2, (half + 1) * SQUARE // 2)
+            nc.vector.transpose(
+                out=both_rows[:, m, :, :].rearrange("p m w e -> p (m w e)").bitcast(F32),
+                in_=seed_repeated[:, m, :].rearrange("p m i -> p (m i)"),
+            )
+
         vision_rows = both_rows[:, :, 0, :]
         bias_rows = both_rows[:, :, 1, :]
 
@@ -107,10 +111,25 @@ def tile_dynamicroutingfusion_pa_s_kernel(tc, text_feat, vision_proj, Wt, bt, ou
             )
             return grouped
 
+        def flip_by_passes(rows):
+            words = rows.bitcast(F32)
+            grouped = stage.tile([P, PASSES * P * PACK], BF16, align_bytes=64)
+            for g in range(PASSES):
+                bank = flip_banks.tile([P, FLIPS, P], F32)
+                for u in range(2):
+                    every_2nd = words[:, g * 2 * P + u : (g + 1) * 2 * P : 2]
+                    nc.tensor.transpose(bank[:, u, :], every_2nd, identity[:])
+                half = slice(g * P * PACK, (g + 1) * P * PACK)
+                nc.scalar.copy(
+                    out=grouped[:, half].bitcast(F32).rearrange("p (r u) -> p r u", u=2),
+                    in_=bank[:, :2, :].rearrange("p u r -> p r u"),
+                )
+            return grouped
+
         grouped_blocks = {}
 
         def flip_block(r):
-            grouped_blocks[r] = flip(w_rows[:, r, :])
+            grouped_blocks[r] = (flip_by_passes if r == BLOCKS - 1 else flip)(w_rows[:, r, :])
 
         def quantise(grouped, codes, scales):
             nc.vector.quantize_mx(out=codes.bitcast(FP8X4), scales=scales, in_=grouped[:])
@@ -170,26 +189,21 @@ def tile_dynamicroutingfusion_pa_s_kernel(tc, text_feat, vision_proj, Wt, bt, ou
                 done = slice(h.stop - STORE, h.stop)
                 nc.sync.dma_start(out=text_proj_out[:, done], in_=text_proj[:, done])
 
+        spread_half(0)
         quantise(flip(x_rows[:]), x_codes[:], x_scales[:])
-        for r in range(4):
+        spread_half(1)
+        for r in range(BLOCKS - 1):
             flip_block(r)
             quantise_block(r)
-        flip_block(4)
-        flip_block(5)
+        flip_block(BLOCKS - 1)
         multiply(0)
         add_coupling(0)
-        quantise_block(4)
-        flip_block(6)
+        quantise_block(BLOCKS - 1)
         multiply(1)
-        quantise_block(5)
         add_coupling(1)
-        flip_block(7)
-        quantise_block(6)
         multiply(2)
         add_coupling(2)
-        quantise_block(7)
         multiply(3)
-        add_coupling(3)
         multiply(4)
 
         early_coupling = keep.tile([P, TOKENS], F32, align_bytes=64)
@@ -199,9 +213,9 @@ def tile_dynamicroutingfusion_pa_s_kernel(tc, text_feat, vision_proj, Wt, bt, ou
             axis=AXIS.X,
             op=ALU.add,
         )
-        add_bias(0)
+        add_coupling(3)
         add_coupling(4)
-        add_bias(1)
+        add_bias(0)
         own_coupling = keep.tile([P, TOKENS], F32, align_bytes=64)
         nc.vector.tensor_scalar(
             out=own_coupling[:],
@@ -211,10 +225,10 @@ def tile_dynamicroutingfusion_pa_s_kernel(tc, text_feat, vision_proj, Wt, bt, ou
             op0=ALU.add,
             op1=ALU.add,
         )
-        add_bias(2)
+        add_bias(1)
         group_coupling = keep.tile([P, TOKENS], F32, align_bytes=64)
         nc.vector.transpose(out=group_coupling[:], in_=own_coupling[:])
-        add_bias(3)
+        add_bias(2)
         minus_max = keep.tile([P, 1], F32)
         nc.vector.tensor_reduce(
             out=minus_max[:], in_=group_coupling[:], axis=AXIS.X, op=ALU.max, negate=True
@@ -226,11 +240,12 @@ def tile_dynamicroutingfusion_pa_s_kernel(tc, text_feat, vision_proj, Wt, bt, ou
         )
         own_exp = keep.tile([P, 1], F32)
         nc.scalar.activation(out=own_exp[:], in_=own_coupling[:, 0:1], func=ACT.Exp, bias=minus_max[:])
+        add_bias(3)
         add_bias(4)
         add_bias(5)
-        add_bias(6)
         one_over_sum = keep.tile([P, 1], F32)
         nc.vector.reciprocal(out=one_over_sum[:], in_=exp_sum[:])
+        add_bias(6)
         add_bias(7)
 
         weighted = keep.tile([P, H], F32)

@@ -50,9 +50,9 @@ def tile_dynamicroutingfusion_pa_s_kernel(tc, text_feat, vision_proj, Wt, bt, ou
         x_rows = keep.tile([P, K], BF16)
         w_rows = keep.tile([P, BLOCKS, K], BF16)
         seed = keep.tile([P, 2, CHUNK], BF16, align_bytes=64)
-        nc.sync.dma_start(out=seed[:, 0, :], in_=vision_proj.rearrange("b o (m e) -> (b o m) e", e=CHUNK))
+        nc.scalar.dma_start(out=seed[:, 0, :], in_=vision_proj.rearrange("b o (m e) -> (b o m) e", e=CHUNK))
         for b in range(BATCH):
-            nc.sync.dma_start(
+            nc.scalar.dma_start(
                 out=seed[b * SQUARE : (b + 1) * SQUARE, 1, :], in_=bt.rearrange("(m e) -> m e", e=CHUNK)
             )
         nc.sync.dma_start(out=x_rows[:], in_=text_rows)
@@ -72,11 +72,17 @@ def tile_dynamicroutingfusion_pa_s_kernel(tc, text_feat, vision_proj, Wt, bt, ou
         nc.scalar.activation(out=table_warmer[:], in_=table_warmer[:], func=ACT.Exp)
 
         seed_flipped = keep.tile([P, SQUARE], F32, align_bytes=64)
-        nc.vector.transpose(out=seed_flipped[:], in_=seed[:].rearrange("p w e -> p (w e)").bitcast(F32))
+
+        def flip_seed():
+            nc.vector.transpose(out=seed_flipped[:], in_=seed[:].rearrange("p w e -> p (w e)").bitcast(F32))
+
         seed_repeated = keep.tile([P, SQUARE, SQUARE], F32, align_bytes=64)
-        nc.vector.tensor_copy(
-            out=seed_repeated[:], in_=seed_flipped[:].unsqueeze(2).to_broadcast([P, SQUARE, SQUARE])
-        )
+
+        def repeat_seed():
+            nc.vector.tensor_copy(
+                out=seed_repeated[:], in_=seed_flipped[:].unsqueeze(2).to_broadcast([P, SQUARE, SQUARE])
+            )
+
         both_rows = keep.tile([P, SQUARE, 2, CHUNK], BF16, align_bytes=64)
 
         def spread_half(half):
@@ -189,10 +195,11 @@ def tile_dynamicroutingfusion_pa_s_kernel(tc, text_feat, vision_proj, Wt, bt, ou
                 done = slice(h.stop - STORE, h.stop)
                 nc.sync.dma_start(out=text_proj_out[:, done], in_=text_proj[:, done])
 
-        spread_half(0)
         quantise(flip(x_rows[:]), x_codes[:], x_scales[:])
-        spread_half(1)
+        spread_steps = [flip_seed, repeat_seed, lambda: spread_half(0), lambda: spread_half(1)]
         for r in range(BLOCKS - 1):
+            if r < len(spread_steps):
+                spread_steps[r]()
             flip_block(r)
             quantise_block(r)
         flip_block(BLOCKS - 1)
@@ -206,20 +213,20 @@ def tile_dynamicroutingfusion_pa_s_kernel(tc, text_feat, vision_proj, Wt, bt, ou
         multiply(3)
         multiply(4)
 
-        early_coupling = keep.tile([P, TOKENS], F32, align_bytes=64)
-        nc.vector.tensor_reduce(
-            out=early_coupling[:],
-            in_=coupling_parts[:, :EARLY].unsqueeze(1).to_broadcast([P, TOKENS, EARLY]),
-            axis=AXIS.X,
-            op=ALU.add,
-        )
+        early_coupling = coupling_parts[:, 0:1].to_broadcast([P, TOKENS])
+        for i in range(1, EARLY):
+            added = keep.tile([P, TOKENS], F32, name=f"added_{i}")
+            nc.scalar.activation(
+                out=added[:], in_=early_coupling, func=ACT.Identity, bias=coupling_parts[:, i : i + 1]
+            )
+            early_coupling = added[:]
         add_coupling(3)
         add_coupling(4)
         add_bias(0)
         own_coupling = keep.tile([P, TOKENS], F32, align_bytes=64)
         nc.vector.tensor_scalar(
             out=own_coupling[:],
-            in0=early_coupling[:],
+            in0=early_coupling,
             scalar1=coupling_parts[:, EARLY : EARLY + 1],
             scalar2=coupling_parts[:, EARLY + 1 : EARLY + 2],
             op0=ALU.add,

from contextlib import ExitStack

import concourse.masks as masks
import concourse.mybir as mybir

F32 = mybir.dt.float32
BF16 = mybir.dt.bfloat16
U32 = mybir.dt.uint32
U8 = mybir.dt.uint8
FP8X4 = mybir.dt.float8_e4m3fn_x4
ALU = mybir.AluOpType
ACT = mybir.ActivationFunctionType
AXIS = mybir.AxisListType

P = 128
BATCH = 4
TOKENS = 32
K = 1024
H = 1024
PACK = 4
PASSES = K // (P * PACK)
WORDS = K // 2
FLIPS = WORDS // P
BLOCKS = H // P
COUPLING_ROUNDS = 2.0
SQUARE = 32
CHUNK = H // SQUARE
LOADS = ((0, 2), (2, 2), (4, 2), (6, 1), (7, 1))
GROUPS = ((0, 2), (2, 2), (4, 2), (6, 1), (7, 1))
EARLY = 3
STORE = 512
WARM_UPS = 3

FLOPS = 2 * P * K * H


def tile_dynamicroutingfusion_pa_s_kernel(tc, text_feat, vision_proj, Wt, bt, out_0, out_1):
    nc = tc.nc
    text_rows = text_feat.rearrange("b l k -> (b l) k")
    text_proj_out = out_0.rearrange("b l h -> (b l) h")
    weighted_out = out_1.rearrange("b l h -> (b l) h")

    with ExitStack() as ctx:
        ctx.enter_context(tc.manual_schedule())
        keep = ctx.enter_context(tc.tile_pool(name="keep", bufs=1))
        stage = ctx.enter_context(tc.tile_pool(name="stage", bufs=4))
        flip_banks = ctx.enter_context(tc.psum_pool(name="flip_banks", bufs=4))
        sum_banks = ctx.enter_context(tc.psum_pool(name="sum_banks", bufs=4))

        x_rows = keep.tile([P, K], BF16)
        w_rows = keep.tile([P, BLOCKS, K], BF16)
        seed = keep.tile([P, 2, CHUNK], BF16, align_bytes=64)
        nc.scalar.dma_start(out=seed[:, 0, :], in_=vision_proj.rearrange("b o (m e) -> (b o m) e", e=CHUNK))
        for b in range(BATCH):
            nc.scalar.dma_start(
                out=seed[b * SQUARE : (b + 1) * SQUARE, 1, :], in_=bt.rearrange("(m e) -> m e", e=CHUNK)
            )
        nc.sync.dma_start(out=x_rows[:], in_=text_rows)
        for first, count in LOADS:
            nc.sync.dma_start(
                out=w_rows[:, first : first + count, :],
                in_=Wt[first * P : (first + count) * P, :].rearrange("(j p) k -> p j k", p=P),
            )

        identity = keep.tile([P, P], F32)
        masks.make_identity(nc, identity[:])
        for warm_up in range(WARM_UPS):
            unread = sum_banks.tile([P, P], F32, tag="sum_bank")
            nc.tensor.matmul(out=unread[:], lhsT=identity[:], rhs=identity[:], start=True, stop=True)
        table_warmer = keep.tile([P, 1], F32)
        nc.vector.memset(table_warmer[:], 0.0)
        nc.scalar.activation(out=table_warmer[:], in_=table_warmer[:], func=ACT.Exp)

        seed_flipped = keep.tile([P, SQUARE], F32, align_bytes=64)

        def flip_seed():
            nc.vector.transpose(out=seed_flipped[:], in_=seed[:].rearrange("p w e -> p (w e)").bitcast(F32))

        seed_repeated = keep.tile([P, SQUARE, SQUARE], F32, align_bytes=64)

        def repeat_seed():
            nc.vector.tensor_copy(
                out=seed_repeated[:], in_=seed_flipped[:].unsqueeze(2).to_broadcast([P, SQUARE, SQUARE])
            )

        both_rows = keep.tile([P, SQUARE, 2, CHUNK], BF16, align_bytes=64)

        def spread_half(half):
            m = slice(half * SQUARE // 2, (half + 1) * SQUARE // 2)
            nc.vector.transpose(
                out=both_rows[:, m, :, :].rearrange("p m w e -> p (m w e)").bitcast(F32),
                in_=seed_repeated[:, m, :].rearrange("p m i -> p (m i)"),
            )

        vision_rows = both_rows[:, :, 0, :]
        bias_rows = both_rows[:, :, 1, :]

        def chunked(columns):
            return columns.rearrange("p (m e) -> p m e", e=CHUNK)

        x_codes = keep.tile([P, PASSES * P], U32, align_bytes=64)
        x_scales = keep.tile([P, PASSES * P], U8, align_bytes=64)
        w_codes = keep.tile([P, BLOCKS, PASSES * P], U32, align_bytes=64)
        w_scales = keep.tile([P, BLOCKS, PASSES * P], U8, align_bytes=64)

        def flip(rows):
            words = rows.bitcast(F32)
            bank = flip_banks.tile([P, FLIPS, P], F32)
            for f in range(FLIPS):
                g, u = divmod(f, 2)
                every_2nd = words[:, g * 2 * P + u : (g + 1) * 2 * P : 2]
                nc.tensor.transpose(bank[:, f, :], every_2nd, identity[:])
            grouped = stage.tile([P, PASSES * P * PACK], BF16, align_bytes=64)
            nc.scalar.copy(
                out=grouped[:].bitcast(F32).rearrange("p (g r u) -> p g r u", g=PASSES, u=2),
                in_=bank[:].rearrange("p (g u) r -> p g r u", u=2),
            )
            return grouped

        def flip_by_passes(rows):
            words = rows.bitcast(F32)
            grouped = stage.tile([P, PASSES * P * PACK], BF16, align_bytes=64)
            for g in range(PASSES):
                bank = flip_banks.tile([P, FLIPS, P], F32)
                for u in range(2):
                    every_2nd = words[:, g * 2 * P + u : (g + 1) * 2 * P : 2]
                    nc.tensor.transpose(bank[:, u, :], every_2nd, identity[:])
                half = slice(g * P * PACK, (g + 1) * P * PACK)
                nc.scalar.copy(
                    out=grouped[:, half].bitcast(F32).rearrange("p (r u) -> p r u", u=2),
                    in_=bank[:, :2, :].rearrange("p u r -> p r u"),
                )
            return grouped

        grouped_blocks = {}

        def flip_block(r):
            grouped_blocks[r] = (flip_by_passes if r == BLOCKS - 1 else flip)(w_rows[:, r, :])

        def quantise(grouped, codes, scales):
            nc.vector.quantize_mx(out=codes.bitcast(FP8X4), scales=scales, in_=grouped[:])

        def quantise_block(r):
            quantise(grouped_blocks[r], w_codes[:, r, :], w_scales[:, r, :])

        text_proj = keep.tile([P, H], F32)
        products = keep.tile([P, H], F32)
        coupling_parts = keep.tile([P, len(GROUPS)], F32)
        group_sums = {}

        def multiply(i):
            first, count = GROUPS[i]
            if i < len(GROUPS) - 1:
                sums = sum_banks.tile([P, count * P], F32, tag="sum_bank")
            else:
                sums = flip_banks.tile([P, count * P], F32, tag="bank")
            for j in range(count):
                for g in range(PASSES):
                    cols = slice(g * P, (g + 1) * P)
                    nc.tensor.matmul_mx(
                        out=sums[:, j * P : (j + 1) * P],
                        lhsT=x_codes[:, cols].bitcast(FP8X4),
                        lhsT_scale=x_scales[:, cols],
                        rhs=w_codes[:, first + j, cols].bitcast(FP8X4),
                        rhs_scale=w_scales[:, first + j, cols],
                        start=(g == 0),
                        stop=(g == PASSES - 1),
                    )
            group_sums[i] = sums

        def add_coupling(i):
            first, count = GROUPS[i]
            h = slice(first * P, (first + count) * P)
            nc.vector.scalar_tensor_tensor(
                out=chunked(products[:, h]),
                in0=chunked(group_sums[i][:]),
                scalar=COUPLING_ROUNDS,
                in1=vision_rows[:, h.start // CHUNK : h.stop // CHUNK, :],
                op0=ALU.mult,
                op1=ALU.mult,
                accum_out=coupling_parts[:, i : i + 1],
            )

        def add_bias(r):
            i = min(r // 2, EARLY) + (r == BLOCKS - 1)
            here = (r - GROUPS[i][0]) * P
            h = slice(r * P, (r + 1) * P)
            nc.vector.tensor_tensor(
                out=chunked(text_proj[:, h]),
                in0=chunked(group_sums[i][:, here : here + P]),
                in1=bias_rows[:, h.start // CHUNK : h.stop // CHUNK, :],
                op=ALU.add,
            )
            if h.stop % STORE == 0:
                done = slice(h.stop - STORE, h.stop)
                nc.sync.dma_start(out=text_proj_out[:, done], in_=text_proj[:, done])

        quantise(flip(x_rows[:]), x_codes[:], x_scales[:])
        spread_steps = [flip_seed, repeat_seed, lambda: spread_half(0), lambda: spread_half(1)]
        for r in range(BLOCKS - 1):
            if r < len(spread_steps):
                spread_steps[r]()
            flip_block(r)
            quantise_block(r)
        flip_block(BLOCKS - 1)
        multiply(0)
        add_coupling(0)
        quantise_block(BLOCKS - 1)
        multiply(1)
        add_coupling(1)
        multiply(2)
        add_coupling(2)
        multiply(3)
        multiply(4)

        early_coupling = coupling_parts[:, 0:1].to_broadcast([P, TOKENS])
        for i in range(1, EARLY):
            added = keep.tile([P, TOKENS], F32, name=f"added_{i}")
            nc.scalar.activation(
                out=added[:], in_=early_coupling, func=ACT.Identity, bias=coupling_parts[:, i : i + 1]
            )
            early_coupling = added[:]
        add_coupling(3)
        add_coupling(4)
        add_bias(0)
        own_coupling = keep.tile([P, TOKENS], F32, align_bytes=64)
        nc.vector.tensor_scalar(
            out=own_coupling[:],
            in0=early_coupling,
            scalar1=coupling_parts[:, EARLY : EARLY + 1],
            scalar2=coupling_parts[:, EARLY + 1 : EARLY + 2],
            op0=ALU.add,
            op1=ALU.add,
        )
        add_bias(1)
        group_coupling = keep.tile([P, TOKENS], F32, align_bytes=64)
        nc.vector.transpose(out=group_coupling[:], in_=own_coupling[:])
        add_bias(2)
        minus_max = keep.tile([P, 1], F32)
        nc.vector.tensor_reduce(
            out=minus_max[:], in_=group_coupling[:], axis=AXIS.X, op=ALU.max, negate=True
        )
        group_exp = keep.tile([P, TOKENS], F32)
        exp_sum = keep.tile([P, 1], F32)
        nc.scalar.activation(
            out=group_exp[:], in_=group_coupling[:], func=ACT.Exp, bias=minus_max[:], accum_out=exp_sum[:]
        )
        own_exp = keep.tile([P, 1], F32)
        nc.scalar.activation(out=own_exp[:], in_=own_coupling[:, 0:1], func=ACT.Exp, bias=minus_max[:])
        add_bias(3)
        add_bias(4)
        add_bias(5)
        one_over_sum = keep.tile([P, 1], F32)
        nc.vector.reciprocal(out=one_over_sum[:], in_=exp_sum[:])
        add_bias(6)
        add_bias(7)

        weighted = keep.tile([P, H], F32)
        for c in range(0, H, STORE):
            nc.vector.tensor_scalar(
                out=chunked(weighted[:, c : c + STORE]),
                in0=vision_rows[:, c // CHUNK : (c + STORE) // CHUNK, :],
                scalar1=own_exp[:],
                scalar2=one_over_sum[:],
                op0=ALU.mult,
                op1=ALU.mult,
            )
            queue = nc.scalar if c else nc.sync
            queue.dma_start(out=weighted_out[:, c : c + STORE], in_=weighted[:, c : c + STORE])
